import numpy as np
import ml_dtypes


def mxq(x, axis, fmt="e4m3"):
    dtype, down = {"e4m3": (ml_dtypes.float8_e4m3fn, 7), "e5m2": (ml_dtypes.float8_e5m2, 14)}[fmt]
    v = np.moveaxis(np.asarray(x, np.float32).astype(ml_dtypes.bfloat16).astype(np.float64), axis, -1)
    blocks = v.reshape(v.shape[:-1] + (-1, 32))
    amax = np.abs(blocks).max(-1, keepdims=True)
    byte = np.maximum(np.where(amax > 0, np.frexp(amax)[1] - 1 + 127, 0) - down, 1)
    scale = np.exp2(byte - 127.0)
    codes = (blocks / scale).astype(np.float32).astype(dtype).astype(np.float64)
    return np.moveaxis((codes * scale).reshape(v.shape), -1, axis)


WIDE = False


def mx_kscale(k):
    if not WIDE:
        return np.ones(k)
    levels = np.array([10, -10, 5, -5, 0])
    a = np.random.permutation(np.resize(levels, k // 512 * 4)).reshape(k // 512, 4)
    idx = np.arange(k)
    return np.exp2(a[idx // 512, idx % 128 // 32])


BF16 = ml_dtypes.bfloat16


def bf(x):
    return np.asarray(x, np.float32).astype(BF16)


def f64(x):
    return np.asarray(x).astype(np.float64)


B, N, D = 4, 512, 512


def setup_inputs():
    s = mx_kscale(D)
    return {"panel_embeddings": bf(np.random.standard_normal((B, N, D)) * s),
            "W": bf(np.random.standard_normal((D, D)) * 4.0 / D / s[:, None] / s[None, :]),
            "b": bf(0.5 + 0.1 * np.random.standard_normal(1))}


def reference(panel_embeddings, W, b):
    xq = mxq(f64(panel_embeddings), 2, "e4m3")
    xw = xq @ mxq(f64(W), 0, "e4m3")
    scores = (mxq(xw, 2, "e4m3") @ xq.transpose(0, 2, 1)) + f64(b)
    n = panel_embeddings.shape[1]
    mask = ~np.eye(n, dtype=bool)
    return np.where(mask, scores, np.zeros_like(scores))

@@ -1,0 +1,189 @@
+from contextlib import ExitStack
+
+import concourse.mybir as mybir
+from concourse.masks import make_identity
+
+F32 = mybir.dt.float32
+BF16 = mybir.dt.bfloat16
+U32 = mybir.dt.uint32
+U8 = mybir.dt.uint8
+FP8X4 = mybir.dt.float8_e4m3fn_x4
+ADD = mybir.AluOpType.add
+MULT = mybir.AluOpType.mult
+
+P = 128
+B, N, D = 4, 512, 512
+RT = N // P
+TILES = B * RT
+FLOPS = 2 * B * N * D * D + 2 * B * N * N * D
+PIN = False
+LAG_F = 1
+LAG_G = 3
+
+
+def tile_readingorderhead_kernel(tc, panel_embeddings, W, b, out):
+    nc = tc.nc
+    with ExitStack() as ctx:
+        keep = ctx.enter_context(tc.tile_pool(name="keep", bufs=1))
+        psum_tr = ctx.enter_context(tc.psum_pool(name="psum_tr", bufs=2))
+        psum_xw = ctx.enter_context(tc.psum_pool(name="psum_xw", bufs=3))
+        psum_sc = ctx.enter_context(tc.psum_pool(name="psum_sc", bufs=3))
+        if PIN:
+            ctx.enter_context(tc.manual_schedule())
+
+        x_sb = [keep.tile([P, RT * D], BF16, name="x_sb%d" % i) for i in range(B)]
+        xg = [keep.tile([P, N * 4], BF16, name="xg%d" % i, align_bytes=64) for i in range(B)]
+        xc = [keep.tile([P, N], U32, name="xc%d" % i, align_bytes=64) for i in range(B)]
+        xs = [keep.tile([P, N], U8, name="xs%d" % i, align_bytes=64) for i in range(B)]
+        xwg = [keep.tile([P, N * 4], BF16, name="xwg%d" % i, align_bytes=64) for i in range(B)]
+        xwc = [keep.tile([P, N], U32, name="xwc%d" % i, align_bytes=64) for i in range(B)]
+        xws = [keep.tile([P, N], U8, name="xws%d" % i, align_bytes=64) for i in range(B)]
+        o_sb = [keep.tile([P, RT, N], F32, name="o_sb%d" % i) for i in range(B)]
+        w_sb = keep.tile([P, 4, D], BF16, name="w_sb")
+        wg = keep.tile([P, D * 4], BF16, name="wg", align_bytes=64)
+        wc = keep.tile([P, D], U32, name="wc", align_bytes=64)
+        ws = keep.tile([P, D], U8, name="ws", align_bytes=64)
+        ident = keep.tile([P, P], F32, name="ident")
+        mask = keep.tile([P, RT, N], F32, name="mask")
+        bias_bf = keep.tile([P, 1], BF16, name="bias_bf")
+        bias = keep.tile([P, 1], F32, name="bias")
+
+        def load_x(bi, r0, r1):
+            nc.sync.dma_start(
+                out=x_sb[bi][:, r0 * D : r1 * D].rearrange("p (r d) -> p r d", d=D),
+                in_=panel_embeddings[bi, r0 * P : r1 * P, :].rearrange("(r p) d -> p r d", p=P),
+            )
+
+        load_x(0, 0, 2)
+        nc.sync.dma_start(
+            out=w_sb[:].rearrange("q (u e) c -> q u (e c)", u=2),
+            in_=W.rearrange("(u q e) c -> q u (e c)", u=2, e=2),
+        )
+        load_x(0, 2, 4)
+        for bi in range(1, B):
+            load_x(bi, 0, RT)
+        nc.scalar.dma_start(out=bias_bf[:], in_=b.partition_broadcast(P))
+
+        make_identity(nc, ident[:])
+        nc.vector.memset(mask[:], 1.0)
+        for r in range(RT):
+            nc.vector.tensor_scalar(
+                out=mask[:, r, P * r : P * r + P], in0=ident[:], scalar1=-1.0, scalar2=1.0, op0=MULT, op1=ADD
+            )
+        nc.vector.tensor_copy(out=bias[:], in_=bias_bf[:])
+
+        def stage_a(bi, h):
+            xt = psum_tr.tile([P, 2, 2, P], F32, name="xt", tag="xt")
+            words = x_sb[bi][:].bitcast(F32)
+            for a in range(2):
+                for u in range(2):
+                    c0 = 256 * (2 * h + a) + P * u
+                    nc.tensor.transpose(xt[:, a, u, :], words[:, c0 : c0 + P], ident[:])
+            return xt
+
+        def stage_b(bi, h, xt):
+            dst = xg[bi][:].bitcast(F32).rearrange("p (h a c u) -> p h a c u", h=2, a=2, u=2)
+            nc.scalar.copy(out=dst[:, h], in_=xt[:].rearrange("p a u c -> p a c u"))
+
+        def stage_c(bi, h):
+            nc.vector.quantize_mx(
+                out=xc[bi][:, 256 * h : 256 * h + 256].bitcast(FP8X4),
+                scales=xs[bi][:, 256 * h : 256 * h + 256],
+                in_=xg[bi][:, 1024 * h : 1024 * h + 1024],
+            )
+
+        def regroup_w(t2, eng):
+            u2, e2 = divmod(t2, 2)
+            src = w_sb[:].rearrange("p t (u q e) -> p u e q t", u=2, e=2)
+            dst = wg[:, 4 * P * t2 : 4 * P * (t2 + 1)].rearrange("p (q t) -> p q t", t=4)
+            if eng == "v":
+                nc.vector.tensor_copy(out=dst, in_=src[:, u2, e2])
+            else:
+                nc.scalar.copy(out=dst, in_=src[:, u2, e2])
+
+        def stage_d(s):
+            bi, r = divmod(s, RT)
+            cols = slice(P * r, P * r + P)
+            pw = psum_xw.tile([P, 4, P], F32, name="pw", tag="pw")
+            for t2 in range(4):
+                nc.tensor.matmul_mx(
+                    out=pw[:, t2, :],
+                    lhsT=wc[:, P * t2 : P * t2 + P].bitcast(FP8X4),
+                    lhsT_scale=ws[:, P * t2 : P * t2 + P],
+                    rhs=xc[bi][:, cols].bitcast(FP8X4),
+                    rhs_scale=xs[bi][:, cols],
+                    start=True,
+                    stop=True,
+                )
+            return pw
+
+        def stage_e(s, pw):
+            bi, r = divmod(s, RT)
+            nc.scalar.copy(
+                out=xwg[bi][:, 512 * r : 512 * r + 512].rearrange("p (i t) -> p i t", t=4),
+                in_=pw[:].rearrange("p t i -> p i t"),
+            )
+
+        def stage_f(s):
+            bi, r = divmod(s, RT)
+            cols = slice(P * r, P * r + P)
+            nc.vector.quantize_mx(
+                out=xwc[bi][:, cols].bitcast(FP8X4),
+                scales=xws[bi][:, cols],
+                in_=xwg[bi][:, 512 * r : 512 * r + 512],
+            )
+
+        def stage_g(s):
+            bi, r = divmod(s, RT)
+            cols = slice(P * r, P * r + P)
+            ps = psum_sc.tile([P, N], F32, name="ps", tag="ps")
+            nc.tensor.matmul_mx(
+                out=ps[:],
+                lhsT=xwc[bi][:, cols].bitcast(FP8X4),
+                lhsT_scale=xws[bi][:, cols],
+                rhs=xc[bi][:].bitcast(FP8X4),
+                rhs_scale=xs[bi][:],
+                start=True,
+                stop=True,
+            )
+            return ps
+
+        def stage_h(s, ps):
+            bi, r = divmod(s, RT)
+            nc.vector.scalar_tensor_tensor(
+                out=o_sb[bi][:, r, :], in0=ps[:], scalar=bias[:, 0:1], in1=mask[:, r, :], op0=ADD, op1=MULT
+            )
+            nc.sync.dma_start(out=out[bi, P * r : P * r + P, :], in_=o_sb[bi][:, r, :])
+
+        xt = stage_a(0, 0)
+        stage_b(0, 0, xt)
+        regroup_w(3, "s")
+        for t2 in range(3):
+            regroup_w(t2, "v")
+        stage_c(0, 0)
+        nc.vector.quantize_mx(out=wc[:].bitcast(FP8X4), scales=ws[:], in_=wg[:])
+        xt = stage_a(0, 1)
+        stage_b(0, 1, xt)
+        stage_c(0, 1)
+
+        xts = {}
+        for s in range(TILES + LAG_G):
+            bi, r = divmod(s, RT)
+            nxt = bi + 1
+            if s < TILES:
+                pw = stage_d(s)
+            if s < TILES and r == 1 and nxt < B:
+                xts[0] = stage_a(nxt, 0)
+                xts[1] = stage_a(nxt, 1)
+            if s >= LAG_G:
+                ps = stage_g(s - LAG_G)
+            if s < TILES:
+                stage_e(s, pw)
+            if s < TILES and nxt < B and r in (1, 2):
+                stage_b(nxt, r - 1, xts[r - 1])
+            if 0 <= s - LAG_F < TILES:
+                stage_f(s - LAG_F)
+            if s < TILES and nxt < B and r in (2, 3):
+                stage_c(nxt, r - 2)
+            if s >= LAG_G:
+                stage_h(s - LAG_G, ps)

@@ -51,7 +51,7 @@ def tile_readingorderhead_kernel(tc, panel_embeddings, W, b, out):
         def load_x(bi, r0, r1):
             nc.sync.dma_start(
                 out=x_sb[bi][:, r0 * D : r1 * D].rearrange("p (r d) -> p r d", d=D),
-                in_=panel_embeddings[bi, r0 * P : r1 * P, :].rearrange("(r p) d -> p r d", p=P),
+                in_=panel_embeddings[bi].rearrange("(p r) d -> p r d", r=RT)[:, r0:r1, :],
             )
 
         load_x(0, 0, 2)
@@ -68,7 +68,7 @@ def tile_readingorderhead_kernel(tc, panel_embeddings, W, b, out):
         nc.vector.memset(mask[:], 1.0)
         for r in range(RT):
             nc.vector.tensor_scalar(
-                out=mask[:, r, P * r : P * r + P], in0=ident[:], scalar1=-1.0, scalar2=1.0, op0=MULT, op1=ADD
+                out=mask[:, r, :].rearrange("p (c q) -> p c q", q=RT)[:, :, r], in0=ident[:], scalar1=-1.0, scalar2=1.0, op0=MULT, op1=ADD
             )
         nc.vector.tensor_copy(out=bias[:], in_=bias_bf[:])
 
@@ -151,9 +151,18 @@ def tile_readingorderhead_kernel(tc, panel_embeddings, W, b, out):
         def stage_h(s, ps):
             bi, r = divmod(s, RT)
             nc.vector.scalar_tensor_tensor(
-                out=o_sb[bi][:, r, :], in0=ps[:], scalar=bias[:, 0:1], in1=mask[:, r, :], op0=ADD, op1=MULT
+                out=o_sb[bi][:, r, :].rearrange("p (c q) -> p c q", q=RT),
+                in0=ps[:].rearrange("p (q c) -> p c q", q=RT),
+                scalar=bias[:, 0:1],
+                in1=mask[:, r, :].rearrange("p (c q) -> p c q", q=RT),
+                op0=ADD,
+                op1=MULT,
             )
-            nc.sync.dma_start(out=out[bi, P * r : P * r + P, :], in_=o_sb[bi][:, r, :])
+            rows = out[bi].rearrange("(c r) j -> c r j", r=RT)
+            if s >= TILES - 2:
+                nc.sync.dma_start(out=rows[:, r : r + 1, :], in_=o_sb[bi][:, r : r + 1, :])
+            elif r % 2 == 1:
+                nc.sync.dma_start(out=rows[:, r - 1 : r + 1, :], in_=o_sb[bi][:, r - 1 : r + 1, :])
 
         xt = stage_a(0, 0)
         stage_b(0, 0, xt)

@@ -10,24 +10,43 @@ U8 = mybir.dt.uint8
 FP8X4 = mybir.dt.float8_e4m3fn_x4
 ADD = mybir.AluOpType.add
 MULT = mybir.AluOpType.mult
+IDENT = mybir.ActivationFunctionType.Identity
 
 P = 128
 B, N, D = 4, 512, 512
 RT = N // P
 TILES = B * RT
 FLOPS = 2 * B * N * D * D + 2 * B * N * N * D
-PIN = False
-LAG_F = 1
-LAG_G = 3
+PIN = True
+WFIRST = False
+OPS = (
+    ("A", 0, "T"), ("B", 0, "S"), ("Wr", 1, "V"), ("Wr", 2, "V"), ("Wr", 3, "S"), ("A", 1, "T"),
+    ("C", 0, "V"), ("Wr", 0, "V"), ("Wq", 0, "V"), ("A", 2, "T"), ("B", 1, "V"), ("D", 0, "T"),
+    ("C", 1, "V"), ("D", 1, "T"), ("B", 2, "S"), ("A", 3, "T"), ("E", 0, "V"), ("E", 1, "S"),
+    ("D", 2, "T"), ("F", 0, "V"), ("C", 2, "V"), ("D", 3, "T"), ("B", 3, "S"), ("F", 1, "V"),
+    ("A", 4, "T"), ("E", 2, "V"), ("E", 3, "S"), ("G", 0, "T"), ("F", 2, "V"), ("C", 3, "V"),
+    ("G", 1, "T"), ("B", 4, "S"), ("F", 3, "V"), ("G", 2, "T"), ("H", 0, "V"), ("D", 4, "T"),
+    ("H", 1, "S"), ("D", 5, "T"), ("C", 4, "V"), ("A", 5, "T"), ("E", 4, "S"), ("H", 2, "V"),
+    ("G", 3, "T"), ("E", 5, "S"), ("F", 4, "V"), ("D", 7, "T"), ("B", 5, "V"), ("D", 6, "T"),
+    ("H", 3, "S"), ("G", 4, "T"), ("C", 5, "V"), ("A", 6, "T"), ("F", 5, "V"), ("E", 7, "S"),
+    ("E", 6, "V"), ("G", 5, "T"), ("H", 4, "S"), ("F", 6, "V"), ("D", 8, "T"), ("F", 7, "V"),
+    ("B", 6, "V"), ("G", 6, "T"), ("H", 5, "S"), ("A", 7, "T"), ("C", 6, "V"), ("E", 8, "S"),
+    ("H", 6, "V"), ("D", 9, "T"), ("D", 10, "T"), ("B", 7, "S"), ("F", 8, "V"), ("D", 11, "T"),
+    ("E", 9, "V"), ("G", 7, "T"), ("E", 10, "S"), ("D", 12, "T"), ("F", 9, "V"), ("E", 11, "V"),
+    ("D", 13, "T"), ("H", 7, "S"), ("G", 9, "T"), ("F", 10, "V"), ("G", 8, "T"), ("F", 11, "V"),
+    ("E", 12, "S"), ("C", 7, "V"), ("G", 11, "T"), ("H", 9, "V"), ("H", 8, "S"), ("G", 10, "T"),
+    ("D", 14, "T"), ("F", 12, "V"), ("E", 13, "V"), ("H", 11, "S"), ("D", 15, "T"), ("G", 12, "T"),
+    ("F", 13, "V"), ("E", 14, "S"), ("H", 10, "V"), ("G", 13, "T"), ("E", 15, "S"), ("F", 14, "V"),
+    ("H", 12, "V"), ("G", 14, "T"), ("H", 13, "S"), ("F", 15, "V"), ("H", 14, "V"), ("G", 15, "T"),
+    ("H", 15, "V"),
+)
 
 
 def tile_readingorderhead_kernel(tc, panel_embeddings, W, b, out):
     nc = tc.nc
     with ExitStack() as ctx:
         keep = ctx.enter_context(tc.tile_pool(name="keep", bufs=1))
-        psum_tr = ctx.enter_context(tc.psum_pool(name="psum_tr", bufs=2))
-        psum_xw = ctx.enter_context(tc.psum_pool(name="psum_xw", bufs=3))
-        psum_sc = ctx.enter_context(tc.psum_pool(name="psum_sc", bufs=3))
+        psum = ctx.enter_context(tc.psum_pool(name="psum", bufs=8))
         if PIN:
             ctx.enter_context(tc.manual_schedule())
 
@@ -47,33 +66,45 @@ def tile_readingorderhead_kernel(tc, panel_embeddings, W, b, out):
         mask = keep.tile([P, RT, N], F32, name="mask")
         bias_bf = keep.tile([P, 1], BF16, name="bias_bf")
         bias = keep.tile([P, 1], F32, name="bias")
+        warm = keep.tile([P, 1], F32, name="warm")
+        warm2 = keep.tile([P, 1], F32, name="warm2")
 
         def load_x(bi, r0, r1):
             nc.sync.dma_start(
                 out=x_sb[bi][:, r0 * D : r1 * D].rearrange("p (r d) -> p r d", d=D),
-                in_=panel_embeddings[bi].rearrange("(p r) d -> p r d", r=RT)[:, r0:r1, :],
+                in_=panel_embeddings[bi, r0 * P : r1 * P, :].rearrange("(r p) d -> p r d", p=P),
             )
 
-        load_x(0, 0, 2)
-        nc.sync.dma_start(
-            out=w_sb[:].rearrange("q (u e) c -> q u (e c)", u=2),
-            in_=W.rearrange("(u q e) c -> q u (e c)", u=2, e=2),
-        )
+        def load_w():
+            nc.sync.dma_start(
+                out=w_sb[:].rearrange("q (u e) c -> q u (e c)", u=2),
+                in_=W.rearrange("(u q e) c -> q u (e c)", u=2, e=2),
+            )
+
+        if WFIRST:
+            load_w()
+            load_x(0, 0, 2)
+        else:
+            load_x(0, 0, 2)
+            load_w()
         load_x(0, 2, 4)
         for bi in range(1, B):
             load_x(bi, 0, RT)
         nc.scalar.dma_start(out=bias_bf[:], in_=b.partition_broadcast(P))
 
+        nc.vector.memset(warm[:], 0.0)
+        nc.scalar.activation(out=warm2[:], in_=warm[:], func=IDENT, bias=warm[:, 0:1], scale=1.0)
         make_identity(nc, ident[:])
         nc.vector.memset(mask[:], 1.0)
         for r in range(RT):
             nc.vector.tensor_scalar(
-                out=mask[:, r, :].rearrange("p (c q) -> p c q", q=RT)[:, :, r], in0=ident[:], scalar1=-1.0, scalar2=1.0, op0=MULT, op1=ADD
+                out=mask[:, r, P * r : P * r + P], in0=ident[:], scalar1=-1.0, scalar2=1.0, op0=MULT, op1=ADD
             )
         nc.vector.tensor_copy(out=bias[:], in_=bias_bf[:])
 
-        def stage_a(bi, h):
-            xt = psum_tr.tile([P, 2, 2, P], F32, name="xt", tag="xt")
+        def stage_a(k):
+            bi, h = divmod(k, 2)
+            xt = psum.tile([P, 2, 2, P], F32, name="xt", tag="bank")
             words = x_sb[bi][:].bitcast(F32)
             for a in range(2):
                 for u in range(2):
@@ -81,11 +112,16 @@ def tile_readingorderhead_kernel(tc, panel_embeddings, W, b, out):
                     nc.tensor.transpose(xt[:, a, u, :], words[:, c0 : c0 + P], ident[:])
             return xt
 
-        def stage_b(bi, h, xt):
+        def stage_b(k, xt, eng):
+            bi, h = divmod(k, 2)
             dst = xg[bi][:].bitcast(F32).rearrange("p (h a c u) -> p h a c u", h=2, a=2, u=2)
-            nc.scalar.copy(out=dst[:, h], in_=xt[:].rearrange("p a u c -> p a c u"))
+            if eng == "V":
+                nc.vector.tensor_copy(out=dst[:, h], in_=xt[:].rearrange("p a u c -> p a c u"))
+            else:
+                nc.scalar.copy(out=dst[:, h], in_=xt[:].rearrange("p a u c -> p a c u"))
 
-        def stage_c(bi, h):
+        def stage_c(k):
+            bi, h = divmod(k, 2)
             nc.vector.quantize_mx(
                 out=xc[bi][:, 256 * h : 256 * h + 256].bitcast(FP8X4),
                 scales=xs[bi][:, 256 * h : 256 * h + 256],
@@ -96,7 +132,7 @@ def tile_readingorderhead_kernel(tc, panel_embeddings, W, b, out):
             u2, e2 = divmod(t2, 2)
             src = w_sb[:].rearrange("p t (u q e) -> p u e q t", u=2, e=2)
             dst = wg[:, 4 * P * t2 : 4 * P * (t2 + 1)].rearrange("p (q t) -> p q t", t=4)
-            if eng == "v":
+            if eng == "V":
                 nc.vector.tensor_copy(out=dst, in_=src[:, u2, e2])
             else:
                 nc.scalar.copy(out=dst, in_=src[:, u2, e2])
@@ -104,7 +140,7 @@ def tile_readingorderhead_kernel(tc, panel_embeddings, W, b, out):
         def stage_d(s):
             bi, r = divmod(s, RT)
             cols = slice(P * r, P * r + P)
-            pw = psum_xw.tile([P, 4, P], F32, name="pw", tag="pw")
+            pw = psum.tile([P, 4, P], F32, name="pw", tag="bank")
             for t2 in range(4):
                 nc.tensor.matmul_mx(
                     out=pw[:, t2, :],
@@ -117,12 +153,13 @@ def tile_readingorderhead_kernel(tc, panel_embeddings, W, b, out):
                 )
             return pw
 
-        def stage_e(s, pw):
+        def stage_e(s, pw, eng):
             bi, r = divmod(s, RT)
-            nc.scalar.copy(
-                out=xwg[bi][:, 512 * r : 512 * r + 512].rearrange("p (i t) -> p i t", t=4),
-                in_=pw[:].rearrange("p t i -> p i t"),
-            )
+            dst = xwg[bi][:, 512 * r : 512 * r + 512].rearrange("p (i t) -> p i t", t=4)
+            if eng == "V":
+                nc.vector.tensor_copy(out=dst, in_=pw[:].rearrange("p t i -> p i t"))
+            else:
+                nc.scalar.copy(out=dst, in_=pw[:].rearrange("p t i -> p i t"))
 
         def stage_f(s):
             bi, r = divmod(s, RT)
@@ -136,7 +173,7 @@ def tile_readingorderhead_kernel(tc, panel_embeddings, W, b, out):
         def stage_g(s):
             bi, r = divmod(s, RT)
             cols = slice(P * r, P * r + P)
-            ps = psum_sc.tile([P, N], F32, name="ps", tag="ps")
+            ps = psum.tile([P, N], F32, name="ps", tag="bank")
             nc.tensor.matmul_mx(
                 out=ps[:],
                 lhsT=xwc[bi][:, cols].bitcast(FP8X4),
@@ -148,51 +185,37 @@ def tile_readingorderhead_kernel(tc, panel_embeddings, W, b, out):
             )
             return ps
 
-        def stage_h(s, ps):
+        def stage_h(s, ps, eng):
             bi, r = divmod(s, RT)
-            nc.vector.scalar_tensor_tensor(
-                out=o_sb[bi][:, r, :].rearrange("p (c q) -> p c q", q=RT),
-                in0=ps[:].rearrange("p (q c) -> p c q", q=RT),
-                scalar=bias[:, 0:1],
-                in1=mask[:, r, :].rearrange("p (c q) -> p c q", q=RT),
-                op0=ADD,
-                op1=MULT,
-            )
-            rows = out[bi].rearrange("(c r) j -> c r j", r=RT)
-            if s >= TILES - 2:
-                nc.sync.dma_start(out=rows[:, r : r + 1, :], in_=o_sb[bi][:, r : r + 1, :])
-            elif r % 2 == 1:
-                nc.sync.dma_start(out=rows[:, r - 1 : r + 1, :], in_=o_sb[bi][:, r - 1 : r + 1, :])
+            if eng == "S":
+                diag = o_sb[bi][:, r, P * r : P * r + P]
+                nc.scalar.activation(out=o_sb[bi][:, r, :], in_=ps[:], func=IDENT, bias=bias[:, 0:1], scale=1.0)
+                nc.gpsimd.tensor_tensor(out=diag, in0=diag, in1=mask[:, r, P * r : P * r + P], op=MULT)
+            else:
+                nc.vector.scalar_tensor_tensor(
+                    out=o_sb[bi][:, r, :], in0=ps[:], scalar=bias[:, 0:1], in1=mask[:, r, :], op0=ADD, op1=MULT
+                )
+            nc.sync.dma_start(out=out[bi, P * r : P * r + P, :], in_=o_sb[bi][:, r, :])
 
-        xt = stage_a(0, 0)
-        stage_b(0, 0, xt)
-        regroup_w(3, "s")
-        for t2 in range(3):
-            regroup_w(t2, "v")
-        stage_c(0, 0)
-        nc.vector.quantize_mx(out=wc[:].bitcast(FP8X4), scales=ws[:], in_=wg[:])
-        xt = stage_a(0, 1)
-        stage_b(0, 1, xt)
-        stage_c(0, 1)
-
-        xts = {}
-        for s in range(TILES + LAG_G):
-            bi, r = divmod(s, RT)
-            nxt = bi + 1
-            if s < TILES:
-                pw = stage_d(s)
-            if s < TILES and r == 1 and nxt < B:
-                xts[0] = stage_a(nxt, 0)
-                xts[1] = stage_a(nxt, 1)
-            if s >= LAG_G:
-                ps = stage_g(s - LAG_G)
-            if s < TILES:
-                stage_e(s, pw)
-            if s < TILES and nxt < B and r in (1, 2):
-                stage_b(nxt, r - 1, xts[r - 1])
-            if 0 <= s - LAG_F < TILES:
-                stage_f(s - LAG_F)
-            if s < TILES and nxt < B and r in (2, 3):
-                stage_c(nxt, r - 2)
-            if s >= LAG_G:
-                stage_h(s - LAG_G, ps)
+        banks = {}
+        for kind, i, eng in OPS:
+            if kind == "A":
+                banks[("A", i)] = stage_a(i)
+            elif kind == "B":
+                stage_b(i, banks[("A", i)], eng)
+            elif kind == "C":
+                stage_c(i)
+            elif kind == "Wr":
+                regroup_w(i, eng)
+            elif kind == "Wq":
+                nc.vector.quantize_mx(out=wc[:].bitcast(FP8X4), scales=ws[:], in_=wg[:])
+            elif kind == "D":
+                banks[("D", i)] = stage_d(i)
+            elif kind == "E":
+                stage_e(i, banks[("D", i)], eng)
+            elif kind == "F":
+                stage_f(i)
+            elif kind == "G":
+                banks[("G", i)] = stage_g(i)
+            else:
+                stage_h(i, banks[("G", i)], eng)

@@ -10,64 +10,52 @@ U8 = mybir.dt.uint8
 FP8X4 = mybir.dt.float8_e4m3fn_x4
 ADD = mybir.AluOpType.add
 MULT = mybir.AluOpType.mult
-IDENT = mybir.ActivationFunctionType.Identity
+IDENTITY = mybir.ActivationFunctionType.Identity
 
 P = 128
 B, N, D = 4, 512, 512
+PACK = 4
 RT = N // P
 TILES = B * RT
+PAIRS = TILES // 2
+BANKS = 8
+LEAD = 2
+XLEAD = 4
 FLOPS = 2 * B * N * D * D + 2 * B * N * N * D
-PIN = True
-WFIRST = False
-OPS = (
-    ("A", 0, "T"), ("B", 0, "S"), ("Wr", 1, "V"), ("Wr", 2, "V"), ("Wr", 3, "S"), ("A", 1, "T"),
-    ("C", 0, "V"), ("Wr", 0, "V"), ("Wq", 0, "V"), ("A", 2, "T"), ("B", 1, "V"), ("D", 0, "T"),
-    ("C", 1, "V"), ("D", 1, "T"), ("B", 2, "S"), ("A", 3, "T"), ("E", 0, "V"), ("E", 1, "S"),
-    ("D", 2, "T"), ("F", 0, "V"), ("C", 2, "V"), ("D", 3, "T"), ("B", 3, "S"), ("F", 1, "V"),
-    ("A", 4, "T"), ("E", 2, "V"), ("E", 3, "S"), ("G", 0, "T"), ("F", 2, "V"), ("C", 3, "V"),
-    ("G", 1, "T"), ("B", 4, "S"), ("F", 3, "V"), ("G", 2, "T"), ("H", 0, "V"), ("D", 4, "T"),
-    ("H", 1, "S"), ("D", 5, "T"), ("C", 4, "V"), ("A", 5, "T"), ("E", 4, "S"), ("H", 2, "V"),
-    ("G", 3, "T"), ("E", 5, "S"), ("F", 4, "V"), ("D", 7, "T"), ("B", 5, "V"), ("D", 6, "T"),
-    ("H", 3, "S"), ("G", 4, "T"), ("C", 5, "V"), ("A", 6, "T"), ("F", 5, "V"), ("E", 7, "S"),
-    ("E", 6, "V"), ("G", 5, "T"), ("H", 4, "S"), ("F", 6, "V"), ("D", 8, "T"), ("F", 7, "V"),
-    ("B", 6, "V"), ("G", 6, "T"), ("H", 5, "S"), ("A", 7, "T"), ("C", 6, "V"), ("E", 8, "S"),
-    ("H", 6, "V"), ("D", 9, "T"), ("D", 10, "T"), ("B", 7, "S"), ("F", 8, "V"), ("D", 11, "T"),
-    ("E", 9, "V"), ("G", 7, "T"), ("E", 10, "S"), ("D", 12, "T"), ("F", 9, "V"), ("E", 11, "V"),
-    ("D", 13, "T"), ("H", 7, "S"), ("G", 9, "T"), ("F", 10, "V"), ("G", 8, "T"), ("F", 11, "V"),
-    ("E", 12, "S"), ("C", 7, "V"), ("G", 11, "T"), ("H", 9, "V"), ("H", 8, "S"), ("G", 10, "T"),
-    ("D", 14, "T"), ("F", 12, "V"), ("E", 13, "V"), ("H", 11, "S"), ("D", 15, "T"), ("G", 12, "T"),
-    ("F", 13, "V"), ("E", 14, "S"), ("H", 10, "V"), ("G", 13, "T"), ("E", 15, "S"), ("F", 14, "V"),
-    ("H", 12, "V"), ("G", 14, "T"), ("H", 13, "S"), ("F", 15, "V"), ("H", 14, "V"), ("G", 15, "T"),
-    ("H", 15, "V"),
-)
 
 
 def tile_readingorderhead_kernel(tc, panel_embeddings, W, b, out):
     nc = tc.nc
     with ExitStack() as ctx:
         keep = ctx.enter_context(tc.tile_pool(name="keep", bufs=1))
-        psum = ctx.enter_context(tc.psum_pool(name="psum", bufs=8))
-        if PIN:
-            ctx.enter_context(tc.manual_schedule())
+        psum = ctx.enter_context(tc.psum_pool(name="psum", bufs=1))
+        ctx.enter_context(tc.manual_schedule())
 
         x_sb = [keep.tile([P, RT * D], BF16, name="x_sb%d" % i) for i in range(B)]
-        xg = [keep.tile([P, N * 4], BF16, name="xg%d" % i, align_bytes=64) for i in range(B)]
+        xg = [keep.tile([P, N * PACK], BF16, name="xg%d" % i, align_bytes=64) for i in range(B)]
         xc = [keep.tile([P, N], U32, name="xc%d" % i, align_bytes=64) for i in range(B)]
         xs = [keep.tile([P, N], U8, name="xs%d" % i, align_bytes=64) for i in range(B)]
-        xwg = [keep.tile([P, N * 4], BF16, name="xwg%d" % i, align_bytes=64) for i in range(B)]
+        xwg = [keep.tile([P, N * PACK], BF16, name="xwg%d" % i, align_bytes=64) for i in range(B)]
         xwc = [keep.tile([P, N], U32, name="xwc%d" % i, align_bytes=64) for i in range(B)]
         xws = [keep.tile([P, N], U8, name="xws%d" % i, align_bytes=64) for i in range(B)]
         o_sb = [keep.tile([P, RT, N], F32, name="o_sb%d" % i) for i in range(B)]
-        w_sb = keep.tile([P, 4, D], BF16, name="w_sb")
-        wg = keep.tile([P, D * 4], BF16, name="wg", align_bytes=64)
+        w_sb = keep.tile([P, PACK, D], BF16, name="w_sb")
+        wg = keep.tile([P, D * PACK], BF16, name="wg", align_bytes=64)
         wc = keep.tile([P, D], U32, name="wc", align_bytes=64)
         ws = keep.tile([P, D], U8, name="ws", align_bytes=64)
         ident = keep.tile([P, P], F32, name="ident")
         mask = keep.tile([P, RT, N], F32, name="mask")
         bias_bf = keep.tile([P, 1], BF16, name="bias_bf")
         bias = keep.tile([P, 1], F32, name="bias")
-        warm = keep.tile([P, 1], F32, name="warm")
-        warm2 = keep.tile([P, 1], F32, name="warm2")
+        zero = keep.tile([P, 1], F32, name="zero")
+        unused = keep.tile([P, 1], F32, name="unused")
+
+        taken = []
+        held = {}
+
+        def next_bank(shape):
+            taken.append(1)
+            return psum.tile(shape, F32, name="acc", tag="bank%d" % ((len(taken) - 1) % BANKS))
 
         def load_x(bi, r0, r1):
             nc.sync.dma_start(
@@ -75,52 +63,22 @@ def tile_readingorderhead_kernel(tc, panel_embeddings, W, b, out):
                 in_=panel_embeddings[bi, r0 * P : r1 * P, :].rearrange("(r p) d -> p r d", p=P),
             )
 
-        def load_w():
-            nc.sync.dma_start(
-                out=w_sb[:].rearrange("q (u e) c -> q u (e c)", u=2),
-                in_=W.rearrange("(u q e) c -> q u (e c)", u=2, e=2),
-            )
-
-        if WFIRST:
-            load_w()
-            load_x(0, 0, 2)
-        else:
-            load_x(0, 0, 2)
-            load_w()
-        load_x(0, 2, 4)
-        for bi in range(1, B):
-            load_x(bi, 0, RT)
-        nc.scalar.dma_start(out=bias_bf[:], in_=b.partition_broadcast(P))
-
-        nc.vector.memset(warm[:], 0.0)
-        nc.scalar.activation(out=warm2[:], in_=warm[:], func=IDENT, bias=warm[:, 0:1], scale=1.0)
-        make_identity(nc, ident[:])
-        nc.vector.memset(mask[:], 1.0)
-        for r in range(RT):
-            nc.vector.tensor_scalar(
-                out=mask[:, r, P * r : P * r + P], in0=ident[:], scalar1=-1.0, scalar2=1.0, op0=MULT, op1=ADD
-            )
-        nc.vector.tensor_copy(out=bias[:], in_=bias_bf[:])
-
-        def stage_a(k):
+        def transpose_half(k):
             bi, h = divmod(k, 2)
-            xt = psum.tile([P, 2, 2, P], F32, name="xt", tag="bank")
+            xt = next_bank([P, 2, 2, P])
             words = x_sb[bi][:].bitcast(F32)
             for a in range(2):
                 for u in range(2):
                     c0 = 256 * (2 * h + a) + P * u
                     nc.tensor.transpose(xt[:, a, u, :], words[:, c0 : c0 + P], ident[:])
-            return xt
+            held[("x", k)] = xt
 
-        def stage_b(k, xt, eng):
+        def copy_half(k):
             bi, h = divmod(k, 2)
             dst = xg[bi][:].bitcast(F32).rearrange("p (h a c u) -> p h a c u", h=2, a=2, u=2)
-            if eng == "V":
-                nc.vector.tensor_copy(out=dst[:, h], in_=xt[:].rearrange("p a u c -> p a c u"))
-            else:
-                nc.scalar.copy(out=dst[:, h], in_=xt[:].rearrange("p a u c -> p a c u"))
+            nc.scalar.copy(out=dst[:, h], in_=held[("x", k)][:].rearrange("p a u c -> p a c u"))
 
-        def stage_c(k):
+        def quantise_half(k):
             bi, h = divmod(k, 2)
             nc.vector.quantize_mx(
                 out=xc[bi][:, 256 * h : 256 * h + 256].bitcast(FP8X4),
@@ -128,20 +86,17 @@ def tile_readingorderhead_kernel(tc, panel_embeddings, W, b, out):
                 in_=xg[bi][:, 1024 * h : 1024 * h + 1024],
             )
 
-        def regroup_w(t2, eng):
+        def regroup_w(t2, copy):
             u2, e2 = divmod(t2, 2)
             src = w_sb[:].rearrange("p t (u q e) -> p u e q t", u=2, e=2)
-            dst = wg[:, 4 * P * t2 : 4 * P * (t2 + 1)].rearrange("p (q t) -> p q t", t=4)
-            if eng == "V":
-                nc.vector.tensor_copy(out=dst, in_=src[:, u2, e2])
-            else:
-                nc.scalar.copy(out=dst, in_=src[:, u2, e2])
+            dst = wg[:, PACK * P * t2 : PACK * P * (t2 + 1)].rearrange("p (q t) -> p q t", t=PACK)
+            copy(out=dst, in_=src[:, u2, e2])
 
-        def stage_d(s):
+        def first_matmul(s):
             bi, r = divmod(s, RT)
             cols = slice(P * r, P * r + P)
-            pw = psum.tile([P, 4, P], F32, name="pw", tag="bank")
-            for t2 in range(4):
+            pw = next_bank([P, PACK, P])
+            for t2 in range(PACK):
                 nc.tensor.matmul_mx(
                     out=pw[:, t2, :],
                     lhsT=wc[:, P * t2 : P * t2 + P].bitcast(FP8X4),
@@ -151,17 +106,16 @@ def tile_readingorderhead_kernel(tc, panel_embeddings, W, b, out):
                     start=True,
                     stop=True,
                 )
-            return pw
+            held[("xw", s)] = pw
 
-        def stage_e(s, pw, eng):
+        def copy_xw(s, copy):
             bi, r = divmod(s, RT)
-            dst = xwg[bi][:, 512 * r : 512 * r + 512].rearrange("p (i t) -> p i t", t=4)
-            if eng == "V":
-                nc.vector.tensor_copy(out=dst, in_=pw[:].rearrange("p t i -> p i t"))
-            else:
-                nc.scalar.copy(out=dst, in_=pw[:].rearrange("p t i -> p i t"))
+            copy(
+                out=xwg[bi][:, 512 * r : 512 * r + 512].rearrange("p (i t) -> p i t", t=PACK),
+                in_=held[("xw", s)][:].rearrange("p t i -> p i t"),
+            )
 
-        def stage_f(s):
+        def quantise_xw(s):
             bi, r = divmod(s, RT)
             cols = slice(P * r, P * r + P)
             nc.vector.quantize_mx(
@@ -170,10 +124,10 @@ def tile_readingorderhead_kernel(tc, panel_embeddings, W, b, out):
                 in_=xwg[bi][:, 512 * r : 512 * r + 512],
             )
 
-        def stage_g(s):
+        def second_matmul(s):
             bi, r = divmod(s, RT)
             cols = slice(P * r, P * r + P)
-            ps = psum.tile([P, N], F32, name="ps", tag="bank")
+            ps = next_bank([P, N])
             nc.tensor.matmul_mx(
                 out=ps[:],
                 lhsT=xwc[bi][:, cols].bitcast(FP8X4),
@@ -183,39 +137,91 @@ def tile_readingorderhead_kernel(tc, panel_embeddings, W, b, out):
                 start=True,
                 stop=True,
             )
-            return ps
+            held[("scores", s)] = ps
 
-        def stage_h(s, ps, eng):
+        def store(s):
             bi, r = divmod(s, RT)
-            if eng == "S":
-                diag = o_sb[bi][:, r, P * r : P * r + P]
-                nc.scalar.activation(out=o_sb[bi][:, r, :], in_=ps[:], func=IDENT, bias=bias[:, 0:1], scale=1.0)
-                nc.gpsimd.tensor_tensor(out=diag, in0=diag, in1=mask[:, r, P * r : P * r + P], op=MULT)
-            else:
-                nc.vector.scalar_tensor_tensor(
-                    out=o_sb[bi][:, r, :], in0=ps[:], scalar=bias[:, 0:1], in1=mask[:, r, :], op0=ADD, op1=MULT
-                )
             nc.sync.dma_start(out=out[bi, P * r : P * r + P, :], in_=o_sb[bi][:, r, :])
 
-        banks = {}
-        for kind, i, eng in OPS:
-            if kind == "A":
-                banks[("A", i)] = stage_a(i)
-            elif kind == "B":
-                stage_b(i, banks[("A", i)], eng)
-            elif kind == "C":
-                stage_c(i)
-            elif kind == "Wr":
-                regroup_w(i, eng)
-            elif kind == "Wq":
-                nc.vector.quantize_mx(out=wc[:].bitcast(FP8X4), scales=ws[:], in_=wg[:])
-            elif kind == "D":
-                banks[("D", i)] = stage_d(i)
-            elif kind == "E":
-                stage_e(i, banks[("D", i)], eng)
-            elif kind == "F":
-                stage_f(i)
-            elif kind == "G":
-                banks[("G", i)] = stage_g(i)
-            else:
-                stage_h(i, banks[("G", i)], eng)
+        def finish_on_vector(s):
+            bi, r = divmod(s, RT)
+            nc.vector.scalar_tensor_tensor(
+                out=o_sb[bi][:, r, :],
+                in0=held[("scores", s)][:],
+                scalar=bias[:, 0:1],
+                in1=mask[:, r, :],
+                op0=ADD,
+                op1=MULT,
+            )
+            store(s)
+
+        def finish_on_scalar(s):
+            bi, r = divmod(s, RT)
+            diag = slice(P * r, P * r + P)
+            nc.scalar.activation(
+                out=o_sb[bi][:, r, :], in_=held[("scores", s)][:], func=IDENTITY, bias=bias[:, 0:1], scale=1.0
+            )
+            nc.gpsimd.tensor_tensor(out=o_sb[bi][:, r, diag], in0=o_sb[bi][:, r, diag], in1=mask[:, r, diag], op=MULT)
+            store(s)
+
+        load_x(0, 0, 2)
+        nc.sync.dma_start(
+            out=w_sb[:].rearrange("q (u e) c -> q u (e c)", u=2),
+            in_=W.rearrange("(u q e) c -> q u (e c)", u=2, e=2),
+        )
+        load_x(0, 2, RT)
+        for bi in range(1, B):
+            load_x(bi, 0, RT)
+        nc.scalar.dma_start(out=bias_bf[:], in_=b.partition_broadcast(P))
+
+        nc.vector.memset(zero[:], 0.0)
+        nc.scalar.activation(out=unused[:], in_=zero[:], func=IDENTITY, bias=zero[:, 0:1], scale=1.0)
+        make_identity(nc, ident[:])
+        nc.vector.memset(mask[:], 1.0)
+        for r in range(RT):
+            nc.vector.tensor_scalar(
+                out=mask[:, r, P * r : P * r + P], in0=ident[:], scalar1=-1.0, scalar2=1.0, op0=MULT, op1=ADD
+            )
+        nc.vector.tensor_copy(out=bias[:], in_=bias_bf[:])
+
+        transpose_half(0)
+        copy_half(0)
+        regroup_w(3, nc.scalar.copy)
+        for t2 in range(3):
+            regroup_w(t2, nc.vector.tensor_copy)
+        quantise_half(0)
+        nc.vector.quantize_mx(out=wc[:].bitcast(FP8X4), scales=ws[:], in_=wg[:])
+        transpose_half(1)
+        copy_half(1)
+        quantise_half(1)
+
+        for m in range(-max(LEAD, XLEAD - 2), PAIRS):
+            ahead = m + LEAD
+            half = m + XLEAD
+            has_half = 2 <= half < 2 * B
+            has_ahead = 0 <= ahead < PAIRS
+            has_pair = m >= 0
+            if has_half:
+                transpose_half(half)
+            if has_ahead:
+                first_matmul(2 * ahead)
+                first_matmul(2 * ahead + 1)
+            if has_pair:
+                second_matmul(2 * m)
+                second_matmul(2 * m + 1)
+            if has_half:
+                copy_half(half)
+            if has_pair:
+                finish_on_scalar(2 * m)
+            if has_ahead:
+                copy_xw(2 * ahead + 1, nc.scalar.copy)
+            if has_ahead:
+                copy_xw(2 * ahead, nc.vector.tensor_copy)
+            if has_half:
+                quantise_half(half)
+            if has_ahead:
+                quantise_xw(2 * ahead)
+            if has_pair:
+                finish_on_vector(2 * m + 1)
+            if has_ahead:
+                quantise_xw(2 * ahead + 1)

@@ -49,6 +49,7 @@ def tile_readingorderhead_kernel(tc, panel_embeddings, W, b, out):
         bias = keep.tile([P, 1], F32, name="bias")
         zero = keep.tile([P, 1], F32, name="zero")
         unused = keep.tile([P, 1], F32, name="unused")
+        warm = keep.tile([P, N], BF16, name="warm")
 
         taken = []
         held = {}
@@ -56,6 +57,11 @@ def tile_readingorderhead_kernel(tc, panel_embeddings, W, b, out):
         def next_bank(shape):
             taken.append(1)
             return psum.tile(shape, F32, name="acc", tag="bank%d" % ((len(taken) - 1) % BANKS))
+
+        def keep_warm(count):
+            sink = next_bank([P, N])
+            for i in range(count):
+                nc.tensor.matmul(out=sink[:], lhsT=warm[:, 0:P], rhs=warm[:], start=True, stop=True)
 
         def load_x(bi, r0, r1):
             nc.sync.dma_start(
@@ -174,6 +180,8 @@ def tile_readingorderhead_kernel(tc, panel_embeddings, W, b, out):
             load_x(bi, 0, RT)
         nc.scalar.dma_start(out=bias_bf[:], in_=b.partition_broadcast(P))
 
+        nc.vector.memset(warm[:], 0.0)
+        keep_warm(5)
         nc.vector.memset(zero[:], 0.0)
         nc.scalar.activation(out=unused[:], in_=zero[:], func=IDENTITY, bias=zero[:, 0:1], scale=1.0)
         make_identity(nc, ident[:])
@@ -185,6 +193,7 @@ def tile_readingorderhead_kernel(tc, panel_embeddings, W, b, out):
         nc.vector.tensor_copy(out=bias[:], in_=bias_bf[:])
 
         transpose_half(0)
+        keep_warm(2)
         copy_half(0)
         regroup_w(3, nc.scalar.copy)
         for t2 in range(3):
@@ -192,6 +201,7 @@ def tile_readingorderhead_kernel(tc, panel_embeddings, W, b, out):
         quantise_half(0)
         nc.vector.quantize_mx(out=wc[:].bitcast(FP8X4), scales=ws[:], in_=wg[:])
         transpose_half(1)
+        keep_warm(2)
         copy_half(1)
         quantise_half(1)
 

from contextlib import ExitStack

import concourse.mybir as mybir
from concourse.masks import make_identity

F32 = mybir.dt.float32
BF16 = mybir.dt.bfloat16
U32 = mybir.dt.uint32
U8 = mybir.dt.uint8
FP8X4 = mybir.dt.float8_e4m3fn_x4
ADD = mybir.AluOpType.add
MULT = mybir.AluOpType.mult
IDENTITY = mybir.ActivationFunctionType.Identity

P = 128
B, N, D = 4, 512, 512
PACK = 4
RT = N // P
TILES = B * RT
PAIRS = TILES // 2
BANKS = 8
LEAD = 2
XLEAD = 4
FLOPS = 2 * B * N * D * D + 2 * B * N * N * D


def tile_readingorderhead_kernel(tc, panel_embeddings, W, b, out):
    nc = tc.nc
    with ExitStack() as ctx:
        keep = ctx.enter_context(tc.tile_pool(name="keep", bufs=1))
        psum = ctx.enter_context(tc.psum_pool(name="psum", bufs=1))
        ctx.enter_context(tc.manual_schedule())

        x_sb = [keep.tile([P, RT * D], BF16, name="x_sb%d" % i) for i in range(B)]
        xg = [keep.tile([P, N * PACK], BF16, name="xg%d" % i, align_bytes=64) for i in range(B)]
        xc = [keep.tile([P, N], U32, name="xc%d" % i, align_bytes=64) for i in range(B)]
        xs = [keep.tile([P, N], U8, name="xs%d" % i, align_bytes=64) for i in range(B)]
        xwg = [keep.tile([P, N * PACK], BF16, name="xwg%d" % i, align_bytes=64) for i in range(B)]
        xwc = [keep.tile([P, N], U32, name="xwc%d" % i, align_bytes=64) for i in range(B)]
        xws = [keep.tile([P, N], U8, name="xws%d" % i, align_bytes=64) for i in range(B)]
        o_sb = [keep.tile([P, RT, N], F32, name="o_sb%d" % i) for i in range(B)]
        w_sb = keep.tile([P, PACK, D], BF16, name="w_sb")
        wg = keep.tile([P, D * PACK], BF16, name="wg", align_bytes=64)
        wc = keep.tile([P, D], U32, name="wc", align_bytes=64)
        ws = keep.tile([P, D], U8, name="ws", align_bytes=64)
        ident = keep.tile([P, P], F32, name="ident")
        mask = keep.tile([P, RT, N], F32, name="mask")
        bias_bf = keep.tile([P, 1], BF16, name="bias_bf")
        bias = keep.tile([P, 1], F32, name="bias")
        zero = keep.tile([P, 1], F32, name="zero")
        unused = keep.tile([P, 1], F32, name="unused")
        warm = keep.tile([P, N], BF16, name="warm")

        taken = []
        held = {}

        def next_bank(shape):
            taken.append(1)
            return psum.tile(shape, F32, name="acc", tag="bank%d" % ((len(taken) - 1) % BANKS))

        def keep_warm(count):
            sink = next_bank([P, N])
            for i in range(count):
                nc.tensor.matmul(out=sink[:], lhsT=warm[:, 0:P], rhs=warm[:], start=True, stop=True)

        def load_x(bi, r0, r1):
            nc.sync.dma_start(
                out=x_sb[bi][:, r0 * D : r1 * D].rearrange("p (r d) -> p r d", d=D),
                in_=panel_embeddings[bi, r0 * P : r1 * P, :].rearrange("(r p) d -> p r d", p=P),
            )

        def transpose_half(k):
            bi, h = divmod(k, 2)
            xt = next_bank([P, 2, 2, P])
            words = x_sb[bi][:].bitcast(F32)
            for a in range(2):
                for u in range(2):
                    c0 = 256 * (2 * h + a) + P * u
                    nc.tensor.transpose(xt[:, a, u, :], words[:, c0 : c0 + P], ident[:])
            held[("x", k)] = xt

        def copy_half(k):
            bi, h = divmod(k, 2)
            dst = xg[bi][:].bitcast(F32).rearrange("p (h a c u) -> p h a c u", h=2, a=2, u=2)
            nc.scalar.copy(out=dst[:, h], in_=held[("x", k)][:].rearrange("p a u c -> p a c u"))

        def quantise_half(k):
            bi, h = divmod(k, 2)
            nc.vector.quantize_mx(
                out=xc[bi][:, 256 * h : 256 * h + 256].bitcast(FP8X4),
                scales=xs[bi][:, 256 * h : 256 * h + 256],
                in_=xg[bi][:, 1024 * h : 1024 * h + 1024],
            )

        def regroup_w(t2, copy):
            u2, e2 = divmod(t2, 2)
            src = w_sb[:].rearrange("p t (u q e) -> p u e q t", u=2, e=2)
            dst = wg[:, PACK * P * t2 : PACK * P * (t2 + 1)].rearrange("p (q t) -> p q t", t=PACK)
            copy(out=dst, in_=src[:, u2, e2])

        def first_matmul(s):
            bi, r = divmod(s, RT)
            cols = slice(P * r, P * r + P)
            pw = next_bank([P, PACK, P])
            for t2 in range(PACK):
                nc.tensor.matmul_mx(
                    out=pw[:, t2, :],
                    lhsT=wc[:, P * t2 : P * t2 + P].bitcast(FP8X4),
                    lhsT_scale=ws[:, P * t2 : P * t2 + P],
                    rhs=xc[bi][:, cols].bitcast(FP8X4),
                    rhs_scale=xs[bi][:, cols],
                    start=True,
                    stop=True,
                )
            held[("xw", s)] = pw

        def copy_xw(s, copy):
            bi, r = divmod(s, RT)
            copy(
                out=xwg[bi][:, 512 * r : 512 * r + 512].rearrange("p (i t) -> p i t", t=PACK),
                in_=held[("xw", s)][:].rearrange("p t i -> p i t"),
            )

        def quantise_xw(s):
            bi, r = divmod(s, RT)
            cols = slice(P * r, P * r + P)
            nc.vector.quantize_mx(
                out=xwc[bi][:, cols].bitcast(FP8X4),
                scales=xws[bi][:, cols],
                in_=xwg[bi][:, 512 * r : 512 * r + 512],
            )

        def second_matmul(s):
            bi, r = divmod(s, RT)
            cols = slice(P * r, P * r + P)
            ps = next_bank([P, N])
            nc.tensor.matmul_mx(
                out=ps[:],
                lhsT=xwc[bi][:, cols].bitcast(FP8X4),
                lhsT_scale=xws[bi][:, cols],
                rhs=xc[bi][:].bitcast(FP8X4),
                rhs_scale=xs[bi][:],
                start=True,
                stop=True,
            )
            held[("scores", s)] = ps

        def store(s):
            bi, r = divmod(s, RT)
            nc.sync.dma_start(out=out[bi, P * r : P * r + P, :], in_=o_sb[bi][:, r, :])

        def finish_on_vector(s):
            bi, r = divmod(s, RT)
            nc.vector.scalar_tensor_tensor(
                out=o_sb[bi][:, r, :],
                in0=held[("scores", s)][:],
                scalar=bias[:, 0:1],
                in1=mask[:, r, :],
                op0=ADD,
                op1=MULT,
            )
            store(s)

        def finish_on_scalar(s):
            bi, r = divmod(s, RT)
            diag = slice(P * r, P * r + P)
            nc.scalar.activation(
                out=o_sb[bi][:, r, :], in_=held[("scores", s)][:], func=IDENTITY, bias=bias[:, 0:1], scale=1.0
            )
            nc.gpsimd.tensor_tensor(out=o_sb[bi][:, r, diag], in0=o_sb[bi][:, r, diag], in1=mask[:, r, diag], op=MULT)
            store(s)

        load_x(0, 0, 2)
        nc.sync.dma_start(
            out=w_sb[:].rearrange("q (u e) c -> q u (e c)", u=2),
            in_=W.rearrange("(u q e) c -> q u (e c)", u=2, e=2),
        )
        load_x(0, 2, RT)
        for bi in range(1, B):
            load_x(bi, 0, RT)
        nc.scalar.dma_start(out=bias_bf[:], in_=b.partition_broadcast(P))

        nc.vector.memset(warm[:], 0.0)
        keep_warm(5)
        nc.vector.memset(zero[:], 0.0)
        nc.scalar.activation(out=unused[:], in_=zero[:], func=IDENTITY, bias=zero[:, 0:1], scale=1.0)
        make_identity(nc, ident[:])
        nc.vector.memset(mask[:], 1.0)
        for r in range(RT):
            nc.vector.tensor_scalar(
                out=mask[:, r, P * r : P * r + P], in0=ident[:], scalar1=-1.0, scalar2=1.0, op0=MULT, op1=ADD
            )
        nc.vector.tensor_copy(out=bias[:], in_=bias_bf[:])

        transpose_half(0)
        keep_warm(2)
        copy_half(0)
        regroup_w(3, nc.scalar.copy)
        for t2 in range(3):
            regroup_w(t2, nc.vector.tensor_copy)
        quantise_half(0)
        nc.vector.quantize_mx(out=wc[:].bitcast(FP8X4), scales=ws[:], in_=wg[:])
        transpose_half(1)
        keep_warm(2)
        copy_half(1)
        quantise_half(1)

        for m in range(-max(LEAD, XLEAD - 2), PAIRS):
            ahead = m + LEAD
            half = m + XLEAD
            has_half = 2 <= half < 2 * B
            has_ahead = 0 <= ahead < PAIRS
            has_pair = m >= 0
            if has_half:
                transpose_half(half)
            if has_ahead:
                first_matmul(2 * ahead)
                first_matmul(2 * ahead + 1)
            if has_pair:
                second_matmul(2 * m)
                second_matmul(2 * m + 1)
            if has_half:
                copy_half(half)
            if has_pair:
                finish_on_scalar(2 * m)
            if has_ahead:
                copy_xw(2 * ahead + 1, nc.scalar.copy)
            if has_ahead:
                copy_xw(2 * ahead, nc.vector.tensor_copy)
            if has_half:
                quantise_half(half)
            if has_ahead:
                quantise_xw(2 * ahead)
            if has_pair:
                finish_on_vector(2 * m + 1)
            if has_ahead:
                quantise_xw(2 * ahead + 1)
